import numpy as np
import ml_dtypes


def mxq(x, axis, fmt="e4m3"):
    dtype, down = {"e4m3": (ml_dtypes.float8_e4m3fn, 7), "e5m2": (ml_dtypes.float8_e5m2, 14)}[fmt]
    v = np.moveaxis(np.asarray(x, np.float32).astype(ml_dtypes.bfloat16).astype(np.float64), axis, -1)
    blocks = v.reshape(v.shape[:-1] + (-1, 32))
    amax = np.abs(blocks).max(-1, keepdims=True)
    byte = np.maximum(np.where(amax > 0, np.frexp(amax)[1] - 1 + 127, 0) - down, 1)
    scale = np.exp2(byte - 127.0)
    codes = (blocks / scale).astype(np.float32).astype(dtype).astype(np.float64)
    return np.moveaxis((codes * scale).reshape(v.shape), -1, axis)


WIDE = False


def mx_kscale(k):
    if not WIDE:
        return np.ones(k)
    levels = np.array([10, -10, 5, -5, 0])
    a = np.random.permutation(np.resize(levels, k // 512 * 4)).reshape(k // 512, 4)
    idx = np.arange(k)
    return np.exp2(a[idx // 512, idx % 128 // 32])


BF16 = ml_dtypes.bfloat16


def bf(x):
    return np.asarray(x, np.float32).astype(BF16)


def f64(x):
    return np.asarray(x).astype(np.float64)


B, H, W, D, X, Y, Z = 512, 64, 4, 8, 16, 16, 16


def setup_inputs():
    s = mx_kscale(B)[:, None, None, None]
    q = np.sqrt(B * W)
    hot = np.zeros(H)
    hot[np.random.permutation(H)[:H // 16]] = 1.5
    ok = (np.random.standard_normal((B, X, Y, Z)) + 4.0 / q) / q
    fk = np.random.standard_normal((B, H, W, D)) / np.sqrt(D) + hot[None, :, None, None] / D
    return {"ok": bf(ok / s), "fk": bf(fk * s)}


def reference(ok, fk):
    ok, fk = f64(ok), f64(fk)
    b, h, w, d = fk.shape
    fsum = fk.sum(axis=-1)
    fq = mxq(fsum.reshape(b, h * w), 0, "e4m3")
    oq = mxq(ok.reshape(b, -1), 0, "e4m3")
    corr = fq.T @ oq
    corr = corr.reshape(b, h, w, -1)
    ak = corr.sum(axis=2)
    avg_ak = ak.mean()
    ak_hat = np.where(ak > avg_ak, ak, 0.0)
    ak_hat = ak_hat - ak_hat.min(axis=1, keepdims=True)
    ak_hat = ak_hat / ak_hat.max(axis=1, keepdims=True)
    return corr, ak_hat

@@ -1,0 +1,220 @@
+from contextlib import ExitStack
+
+import concourse.mybir as mybir
+
+FLOPS = 2 * 512 * 256 * 4096
+
+F32 = mybir.dt.float32
+BF16 = mybir.dt.bfloat16
+U32 = mybir.dt.uint32
+U8 = mybir.dt.uint8
+FP8X4 = mybir.dt.float8_e4m3fn_x4
+ALU = mybir.AluOpType
+ACT = mybir.ActivationFunctionType
+AX = mybir.AxisListType
+
+P = 128
+PACK = 4
+CH = 512
+NCH = 8
+
+FK_UNITS = (512, 512, 1024)
+OK_UNITS = (1024, 1024, 1024, 512, 512)
+
+
+def tile_correlationblock_t_kernel(tc, ok, fk, out_0, out_1):
+    nc = tc.nc
+    ok_v = ok.rearrange("(p j) x y z -> p j (x y z)", j=PACK)
+    fk_v = fk.rearrange("(p j) h w d -> p j (h w d)", j=PACK)
+    corr_v = out_0.rearrange("(r s) h w k -> r (s h w k)", s=2)
+    hat_v = out_1.rearrange("(r s) h k -> r (s h k)", s=2)
+
+    with ExitStack() as ctx:
+        keep = ctx.enter_context(tc.tile_pool(name="keep", bufs=1))
+        ps_ak = ctx.enter_context(tc.psum_pool(name="ps_ak", bufs=1))
+        ps_c = ctx.enter_context(tc.psum_pool(name="ps_c", bufs=4))
+        ctx.enter_context(tc.manual_schedule())
+
+        ones = keep.tile([P, P], F32)
+        nc.vector.memset(ones[:], 1.0 / 262144.0)
+
+        fk_at = {}
+        ok_at = {}
+
+        def load(view, units, u, table, step, nm):
+            lo = sum(units[:u])
+            t = keep.tile([P, PACK, units[u]], BF16, name="%s%d" % (nm, u))
+            nc.sync.dma_start(out=t[:], in_=view[:, :, lo:lo + units[u]])
+            for i in range(units[u] // step):
+                table[lo // step + i] = t[:, :, i * step:(i + 1) * step]
+
+        load(fk_v, FK_UNITS, 0, fk_at, 512, "fk_raw")
+        load(fk_v, FK_UNITS, 1, fk_at, 512, "fk_raw")
+        load(ok_v, OK_UNITS, 0, ok_at, CH, "ok_raw")
+        load(fk_v, FK_UNITS, 2, fk_at, 512, "fk_raw")
+        for u in range(1, 5):
+            load(ok_v, OK_UNITS, u, ok_at, CH, "ok_raw")
+
+        fgrp = keep.tile([P, 256, PACK], BF16, align_bytes=64)
+        f_codes = keep.tile([P, 256], U32, align_bytes=64)
+        f_scales = keep.tile([P, 256], U8, align_bytes=64)
+        o_codes = keep.tile([P, NCH * CH], U32, align_bytes=64)
+        o_scales = keep.tile([P, NCH * CH], U8, align_bytes=64)
+        grp = [keep.tile([P, CH, PACK], BF16, name="grp%d" % c, align_bytes=64) for c in range(NCH)]
+        corr_sb = [keep.tile([P, NCH * CH], F32, name="corr_sb%d" % mt) for mt in range(2)]
+        ak_sb = [keep.tile([P, 1024], F32, name="ak_sb%d" % mt) for mt in range(2)]
+        ak_ps = [[ps_ak.tile([P, 512], F32, name="ak_ps%d%d" % (mt, s)) for s in range(2)] for mt in range(2)]
+        rowsum = keep.tile([P, 4], F32)
+        avg = keep.tile([P, 1], F32)
+
+        def fsum(q):
+            with nc.allow_low_precision(reason="float32 sum, rounded once to bfloat16 as the task says"):
+                nc.vector.tensor_reduce(
+                    out=fgrp[:, q * 64:(q + 1) * 64, :].rearrange("p g j -> p j g"),
+                    in_=fk_at[q].rearrange("p j (g d) -> p j g d", d=8), axis=AX.X, op=ALU.add)
+
+        def quant_f(mt):
+            nc.vector.quantize_mx(
+                out=f_codes[:, mt * P:(mt + 1) * P].bitcast(FP8X4), scales=f_scales[:, mt * P:(mt + 1) * P],
+                in_=fgrp[:, mt * P:(mt + 1) * P, :].rearrange("p g j -> p (g j)"))
+
+        def regroup(c, eng):
+            src = ok_at[c].rearrange("p j (h w k) -> p w h j k", w=4, k=8)
+            dst = grp[c][:].rearrange("p (w h k) j -> p w h j k", w=4, k=8)
+            if eng == "v":
+                nc.vector.tensor_copy(out=dst, in_=src)
+            for w in range(4):
+                if eng == "s":
+                    nc.scalar.copy(out=dst[:, w], in_=src[:, w])
+                if eng == "g":
+                    nc.gpsimd.tensor_scalar(out=dst[:, w], in0=src[:, w], scalar1=1.0, scalar2=0.0, op0=ALU.mult, op1=ALU.add)
+
+        def quant(c):
+            nc.vector.quantize_mx(
+                out=o_codes[:, c * CH:(c + 1) * CH].bitcast(FP8X4), scales=o_scales[:, c * CH:(c + 1) * CH],
+                in_=grp[c][:].rearrange("p c j -> p (c j)"))
+
+        def mx(out, mt, lo, n, start, stop):
+            nc.tensor.matmul_mx(
+                out=out, lhsT=f_codes[:, mt * P:(mt + 1) * P].bitcast(FP8X4), lhsT_scale=f_scales[:, mt * P:(mt + 1) * P],
+                rhs=o_codes[:, lo:lo + n].bitcast(FP8X4), rhs_scale=o_scales[:, lo:lo + n], start=start, stop=stop)
+
+        def ak_passes(c):
+            for mt in range(2):
+                for w in range(4):
+                    mx(ak_ps[mt][c // 4][:, (c % 4) * P:(c % 4 + 1) * P], mt, c * CH + w * P, P, w == 0, w == 3)
+
+        def ak_out(mt, s):
+            nc.scalar.activation(out=ak_sb[mt][:, s * 512:(s + 1) * 512], in_=ak_ps[mt][s][:], func=ACT.Copy,
+                                 accum_out=rowsum[:, 2 * s + mt:2 * s + mt + 1])
+
+        banks = {}
+
+        def corr_pass(c, mt):
+            acc = ps_c.tile([P, CH], F32, name="acc")
+            banks[(c, mt)] = acc
+            mx(acc[:], mt, c * CH, CH, True, True)
+
+        def corr_out(c, mt):
+            nc.scalar.copy(
+                out=corr_sb[mt][:, c * CH:(c + 1) * CH].rearrange("p (h w k) -> p h w k", w=4, k=8),
+                in_=banks[(c, mt)][:].rearrange("p (w h k) -> p h w k", w=4, k=8))
+            if c % 2 == 1:
+                nc.sync.dma_start(out=corr_v[mt * P:(mt + 1) * P, (c - 1) * CH:(c + 1) * CH],
+                                  in_=corr_sb[mt][:, (c - 1) * CH:(c + 1) * CH])
+
+        jobs = [(c, mt) for c in range(NCH) for mt in range(2)]
+
+        fsum(0)
+        fsum(1)
+        regroup(0, "s")
+        regroup(1, "g")
+        quant_f(0)
+        fsum(2)
+        fsum(3)
+        regroup(2, "s")
+        regroup(3, "g")
+        quant_f(1)
+        quant(0)
+        quant(1)
+        ak_passes(0)
+        ak_passes(1)
+        regroup(4, "s")
+        quant(2)
+        quant(3)
+        ak_passes(2)
+        ak_passes(3)
+        for i in range(4):
+            corr_pass(*jobs[i])
+        regroup(5, "v")
+        quant(4)
+        quant(5)
+        ak_passes(4)
+        ak_passes(5)
+        regroup(6, "s")
+        ak_out(0, 0)
+        ak_out(1, 0)
+        regroup(7, "v")
+        quant(6)
+        quant(7)
+        ak_passes(6)
+        ak_passes(7)
+        for i in range(3):
+            corr_out(*jobs[i])
+        ak_out(0, 1)
+        ak_out(1, 1)
+
+        mean_ps = ps_c.tile([P, CH], F32, name="acc")
+        nc.tensor.matmul(out=mean_ps[:, 0:4], lhsT=ones[:], rhs=rowsum[:], start=True, stop=True)
+        nc.vector.tensor_reduce(out=avg[:], in_=mean_ps[:, 0:4], axis=AX.X, op=ALU.add)
+
+        for i in range(3, 16):
+            if i + 1 < 16:
+                corr_pass(*jobs[i + 1])
+            corr_out(*jobs[i])
+
+        pieces = [(0, 0), (1, 0), (0, 1), (1, 1)]
+        m = [keep.tile([P, 512], F32, name="m%d" % i) for i in range(4)]
+        hat = [keep.tile([P, 512], F32, name="hat%d" % i) for i in range(4)]
+        mn = [keep.tile([P, 8], F32, name="mn%d" % i) for i in range(4)]
+        mxm = [keep.tile([P, 8], F32, name="mxm%d" % i) for i in range(4)]
+        inv = [keep.tile([P, 8], F32, name="inv%d" % i) for i in range(4)]
+
+        def select(i):
+            mt, s = pieces[i]
+            nc.vector.scalar_tensor_tensor(out=m[i][:], in0=ak_ps[mt][s][:], scalar=avg[:, 0:1],
+                                           in1=ak_sb[mt][:, s * 512:(s + 1) * 512], op0=ALU.is_gt, op1=ALU.mult)
+
+        def minmax(i):
+            m_kh = m[i][:].rearrange("p (h k) -> p k h", k=8)
+            nc.vector.tensor_reduce(out=mn[i][:], in_=m_kh, axis=AX.X, op=ALU.min)
+            nc.vector.tensor_reduce(out=mxm[i][:], in_=m_kh, axis=AX.X, op=ALU.max)
+
+        def small(i):
+            nc.vector.tensor_tensor(out=inv[i][:], in0=mxm[i][:], in1=mn[i][:], op=ALU.subtract)
+            nc.vector.reciprocal(out=inv[i][:], in_=inv[i][:])
+
+        def norm(i, eng, queue):
+            mt, s = pieces[i]
+            m_hk = m[i][:].rearrange("p (h k) -> p h k", k=8)
+            eng.tensor_tensor(out=m_hk, in0=m_hk, in1=mn[i][:].unsqueeze(1).to_broadcast([P, 64, 8]), op=ALU.subtract)
+            eng.tensor_tensor(out=hat[i][:].rearrange("p (h k) -> p h k", k=8), in0=m_hk,
+                              in1=inv[i][:].unsqueeze(1).to_broadcast([P, 64, 8]), op=ALU.mult)
+            queue.dma_start(out=hat_v[mt * P:(mt + 1) * P, s * 512:(s + 1) * 512], in_=hat[i][:])
+
+        select(0)
+        minmax(0)
+        select(1)
+        small(0)
+        norm(0, nc.gpsimd, nc.gpsimd)
+        minmax(1)
+        select(2)
+        small(1)
+        norm(1, nc.gpsimd, nc.gpsimd)
+        minmax(2)
+        select(3)
+        small(2)
+        minmax(3)
+        norm(2, nc.vector, nc.sync)
+        small(3)
+        norm(3, nc.vector, nc.sync)

@@ -64,7 +64,7 @@ def tile_correlationblock_t_kernel(tc, ok, fk, out_0, out_1):
         corr_sb = [keep.tile([P, NCH * CH], F32, name="corr_sb%d" % mt) for mt in range(2)]
         ak_sb = [keep.tile([P, 1024], F32, name="ak_sb%d" % mt) for mt in range(2)]
         ak_ps = [[ps_ak.tile([P, 512], F32, name="ak_ps%d%d" % (mt, s)) for s in range(2)] for mt in range(2)]
-        rowsum = keep.tile([P, 4], F32)
+        rowsum = keep.tile([P, 6], F32)
         avg = keep.tile([P, 1], F32)
 
         def fsum(q):
@@ -104,9 +104,11 @@ def tile_correlationblock_t_kernel(tc, ok, fk, out_0, out_1):
                 for w in range(4):
                     mx(ak_ps[mt][c // 4][:, (c % 4) * P:(c % 4 + 1) * P], mt, c * CH + w * P, P, w == 0, w == 3)
 
-        def ak_out(mt, s):
-            nc.scalar.activation(out=ak_sb[mt][:, s * 512:(s + 1) * 512], in_=ak_ps[mt][s][:], func=ACT.Copy,
-                                 accum_out=rowsum[:, 2 * s + mt:2 * s + mt + 1])
+        def ak_out(mt, s, h0, h1, col):
+            nc.scalar.activation(
+                out=ak_sb[mt][:, s * 512:(s + 1) * 512].rearrange("p (k h) -> p k h", k=8)[:, :, h0:h1],
+                in_=ak_ps[mt][s][:].rearrange("p (h k) -> p k h", k=8)[:, :, h0:h1], func=ACT.Copy,
+                accum_out=rowsum[:, col:col + 1])
 
         banks = {}
 
@@ -152,8 +154,10 @@ def tile_correlationblock_t_kernel(tc, ok, fk, out_0, out_1):
         ak_passes(4)
         ak_passes(5)
         regroup(6, "s")
-        ak_out(0, 0)
-        ak_out(1, 0)
+        ak_out(0, 0, 0, 64, 0)
+        ak_out(1, 0, 0, 64, 1)
+        ak_out(0, 1, 0, 32, 2)
+        ak_out(1, 1, 0, 32, 3)
         regroup(7, "v")
         quant(6)
         quant(7)
@@ -161,12 +165,12 @@ def tile_correlationblock_t_kernel(tc, ok, fk, out_0, out_1):
         ak_passes(7)
         for i in range(3):
             corr_out(*jobs[i])
-        ak_out(0, 1)
-        ak_out(1, 1)
+        ak_out(0, 1, 32, 64, 4)
+        ak_out(1, 1, 32, 64, 5)
 
         mean_ps = ps_c.tile([P, CH], F32, name="acc")
-        nc.tensor.matmul(out=mean_ps[:, 0:4], lhsT=ones[:], rhs=rowsum[:], start=True, stop=True)
-        nc.vector.tensor_reduce(out=avg[:], in_=mean_ps[:, 0:4], axis=AX.X, op=ALU.add)
+        nc.tensor.matmul(out=mean_ps[:, 0:6], lhsT=ones[:], rhs=rowsum[:], start=True, stop=True)
+        nc.vector.tensor_reduce(out=avg[:], in_=mean_ps[:, 0:6], axis=AX.X, op=ALU.add)
 
         for i in range(3, 16):
             if i + 1 < 16:
@@ -182,11 +186,13 @@ def tile_correlationblock_t_kernel(tc, ok, fk, out_0, out_1):
 
         def select(i):
             mt, s = pieces[i]
-            nc.vector.scalar_tensor_tensor(out=m[i][:], in0=ak_ps[mt][s][:], scalar=avg[:, 0:1],
-                                           in1=ak_sb[mt][:, s * 512:(s + 1) * 512], op0=ALU.is_gt, op1=ALU.mult)
+            nc.vector.scalar_tensor_tensor(
+                out=m[i][:].rearrange("p (k h) -> p k h", k=8), in0=ak_ps[mt][s][:].rearrange("p (h k) -> p k h", k=8),
+                scalar=avg[:, 0:1], in1=ak_sb[mt][:, s * 512:(s + 1) * 512].rearrange("p (k h) -> p k h", k=8),
+                op0=ALU.is_gt, op1=ALU.mult)
 
         def minmax(i):
-            m_kh = m[i][:].rearrange("p (h k) -> p k h", k=8)
+            m_kh = m[i][:].rearrange("p (k h) -> p k h", k=8)
             nc.vector.tensor_reduce(out=mn[i][:], in_=m_kh, axis=AX.X, op=ALU.min)
             nc.vector.tensor_reduce(out=mxm[i][:], in_=m_kh, axis=AX.X, op=ALU.max)
 
@@ -196,10 +202,11 @@ def tile_correlationblock_t_kernel(tc, ok, fk, out_0, out_1):
 
         def norm(i, eng, queue):
             mt, s = pieces[i]
-            m_hk = m[i][:].rearrange("p (h k) -> p h k", k=8)
-            eng.tensor_tensor(out=m_hk, in0=m_hk, in1=mn[i][:].unsqueeze(1).to_broadcast([P, 64, 8]), op=ALU.subtract)
-            eng.tensor_tensor(out=hat[i][:].rearrange("p (h k) -> p h k", k=8), in0=m_hk,
-                              in1=inv[i][:].unsqueeze(1).to_broadcast([P, 64, 8]), op=ALU.mult)
+            m_kh = m[i][:].rearrange("p (k h) -> p k h", k=8)
+            eng.tensor_tensor(out=m_kh, in0=m_kh, in1=mn[i][:].unsqueeze(2).to_broadcast([P, 8, 64]), op=ALU.subtract)
+            eng.tensor_tensor(out=hat[i][:].rearrange("p (b i k) -> p b k i", i=4, k=8),
+                              in0=m[i][:].rearrange("p (k b i) -> p b k i", k=8, i=4),
+                              in1=inv[i][:].unsqueeze(1).unsqueeze(3).to_broadcast([P, 16, 8, 4]), op=ALU.mult)
             queue.dma_start(out=hat_v[mt * P:(mt + 1) * P, s * 512:(s + 1) * 512], in_=hat[i][:])
 
         select(0)

@@ -18,7 +18,7 @@ PACK = 4
 CH = 512
 NCH = 8
 
-FK_UNITS = (512, 512, 1024)
+FK_UNITS = (512, 512, 512, 512)
 OK_UNITS = (1024, 1024, 1024, 512, 512)
 
 
@@ -50,8 +50,9 @@ def tile_correlationblock_t_kernel(tc, ok, fk, out_0, out_1):
 
         load(fk_v, FK_UNITS, 0, fk_at, 512, "fk_raw")
         load(fk_v, FK_UNITS, 1, fk_at, 512, "fk_raw")
-        load(ok_v, OK_UNITS, 0, ok_at, CH, "ok_raw")
         load(fk_v, FK_UNITS, 2, fk_at, 512, "fk_raw")
+        load(ok_v, OK_UNITS, 0, ok_at, CH, "ok_raw")
+        load(fk_v, FK_UNITS, 3, fk_at, 512, "fk_raw")
         for u in range(1, 5):
             load(ok_v, OK_UNITS, u, ok_at, CH, "ok_raw")
 
@@ -117,8 +118,8 @@ def tile_correlationblock_t_kernel(tc, ok, fk, out_0, out_1):
             banks[(c, mt)] = acc
             mx(acc[:], mt, c * CH, CH, True, True)
 
-        def corr_out(c, mt):
-            nc.scalar.copy(
+        def corr_out(c, mt, eng=None):
+            (eng or nc.scalar.copy)(
                 out=corr_sb[mt][:, c * CH:(c + 1) * CH].rearrange("p (h w k) -> p h w k", w=4, k=8),
                 in_=banks[(c, mt)][:].rearrange("p (w h k) -> p h w k", w=4, k=8))
             if c % 2 == 1:
@@ -129,42 +130,45 @@ def tile_correlationblock_t_kernel(tc, ok, fk, out_0, out_1):
 
         fsum(0)
         fsum(1)
+        fsum(2)
         regroup(0, "s")
         regroup(1, "g")
         quant_f(0)
-        fsum(2)
         fsum(3)
-        regroup(2, "s")
-        regroup(3, "g")
         quant_f(1)
         quant(0)
-        quant(1)
         ak_passes(0)
+        regroup(2, "s")
+        regroup(3, "v")
+        quant(1)
         ak_passes(1)
-        regroup(4, "s")
-        quant(2)
         quant(3)
-        ak_passes(2)
         ak_passes(3)
+        regroup(4, "s")
+        regroup(5, "v")
+        quant(2)
+        ak_passes(2)
         for i in range(4):
             corr_pass(*jobs[i])
-        regroup(5, "v")
-        quant(4)
         quant(5)
-        ak_passes(4)
         ak_passes(5)
         regroup(6, "s")
+        regroup(7, "v")
+        quant(4)
+        ak_passes(4)
+        quant(7)
+        ak_passes(7)
         ak_out(0, 0, 0, 64, 0)
         ak_out(1, 0, 0, 64, 1)
         ak_out(0, 1, 0, 32, 2)
         ak_out(1, 1, 0, 32, 3)
-        regroup(7, "v")
         quant(6)
-        quant(7)
         ak_passes(6)
-        ak_passes(7)
-        for i in range(3):
-            corr_out(*jobs[i])
+        corr_out(*jobs[0], eng=nc.vector.tensor_copy)
+        corr_pass(*jobs[4])
+        corr_out(*jobs[1], eng=nc.vector.tensor_copy)
+        corr_pass(*jobs[5])
+        corr_out(*jobs[2], eng=nc.vector.tensor_copy)
         ak_out(0, 1, 32, 64, 4)
         ak_out(1, 1, 32, 64, 5)
 
@@ -172,10 +176,15 @@ def tile_correlationblock_t_kernel(tc, ok, fk, out_0, out_1):
         nc.tensor.matmul(out=mean_ps[:, 0:6], lhsT=ones[:], rhs=rowsum[:], start=True, stop=True)
         nc.vector.tensor_reduce(out=avg[:], in_=mean_ps[:, 0:6], axis=AX.X, op=ALU.add)
 
+        nxt = 6
         for i in range(3, 16):
-            if i + 1 < 16:
-                corr_pass(*jobs[i + 1])
             corr_out(*jobs[i])
+            if nxt < 16:
+                corr_pass(*jobs[nxt])
+                nxt += 1
+            if i == 5:
+                corr_pass(*jobs[nxt])
+                nxt += 1
 
         pieces = [(0, 0), (1, 0), (0, 1), (1, 1)]
         m = [keep.tile([P, 512], F32, name="m%d" % i) for i in range(4)]

@@ -226,8 +226,8 @@ def tile_correlationblock_t_kernel(tc, ok, fk, out_0, out_1):
         minmax(1)
         select(2)
         small(1)
-        norm(1, nc.gpsimd, nc.gpsimd)
         minmax(2)
+        norm(1, nc.vector, nc.sync)
         select(3)
         small(2)
         minmax(3)

@@ -138,18 +138,24 @@ def tile_correlationblock_t_kernel(tc, ok, fk, out_0, out_1):
         quant_f(1)
         quant(0)
         ak_passes(0)
-        regroup(2, "s")
+        corr_pass(*jobs[0])
+        corr_pass(*jobs[1])
+        regroup(2, "g")
         regroup(3, "v")
         quant(1)
         ak_passes(1)
+        corr_pass(*jobs[2])
+        corr_pass(*jobs[3])
+        corr_out(*jobs[0])
+        corr_out(*jobs[1])
         quant(3)
         ak_passes(3)
         regroup(4, "s")
         regroup(5, "v")
         quant(2)
         ak_passes(2)
-        for i in range(4):
-            corr_pass(*jobs[i])
+        corr_pass(*jobs[4])
+        corr_pass(*jobs[5])
         quant(5)
         ak_passes(5)
         regroup(6, "s")
@@ -164,11 +170,11 @@ def tile_correlationblock_t_kernel(tc, ok, fk, out_0, out_1):
         ak_out(1, 1, 0, 32, 3)
         quant(6)
         ak_passes(6)
-        corr_out(*jobs[0], eng=nc.vector.tensor_copy)
-        corr_pass(*jobs[4])
-        corr_out(*jobs[1], eng=nc.vector.tensor_copy)
-        corr_pass(*jobs[5])
         corr_out(*jobs[2], eng=nc.vector.tensor_copy)
+        corr_pass(*jobs[6])
+        corr_out(*jobs[3], eng=nc.vector.tensor_copy)
+        corr_pass(*jobs[7])
+        corr_out(*jobs[4], eng=nc.vector.tensor_copy)
         ak_out(0, 1, 32, 64, 4)
         ak_out(1, 1, 32, 64, 5)
 
@@ -176,61 +182,69 @@ def tile_correlationblock_t_kernel(tc, ok, fk, out_0, out_1):
         nc.tensor.matmul(out=mean_ps[:, 0:6], lhsT=ones[:], rhs=rowsum[:], start=True, stop=True)
         nc.vector.tensor_reduce(out=avg[:], in_=mean_ps[:, 0:6], axis=AX.X, op=ALU.add)
 
-        nxt = 6
-        for i in range(3, 16):
+        nxt = 8
+        for i in range(5, 16):
             corr_out(*jobs[i])
             if nxt < 16:
                 corr_pass(*jobs[nxt])
                 nxt += 1
-            if i == 5:
+            if i == 7:
                 corr_pass(*jobs[nxt])
                 nxt += 1
 
         pieces = [(0, 0), (1, 0), (0, 1), (1, 1)]
-        m = [keep.tile([P, 512], F32, name="m%d" % i) for i in range(4)]
+        m = [keep.tile([P, 1024], F32, name="m%d" % i) for i in range(2)]
         hat = [keep.tile([P, 512], F32, name="hat%d" % i) for i in range(4)]
-        mn = [keep.tile([P, 8], F32, name="mn%d" % i) for i in range(4)]
-        mxm = [keep.tile([P, 8], F32, name="mxm%d" % i) for i in range(4)]
-        inv = [keep.tile([P, 8], F32, name="inv%d" % i) for i in range(4)]
+        mn = [keep.tile([P, 16], F32, name="mn%d" % i) for i in range(2)]
+        mxm = [keep.tile([P, 16], F32, name="mxm%d" % i) for i in range(2)]
+        inv = [keep.tile([P, 16], F32, name="inv%d" % i) for i in range(2)]
 
         def select(i):
             mt, s = pieces[i]
             nc.vector.scalar_tensor_tensor(
-                out=m[i][:].rearrange("p (k h) -> p k h", k=8), in0=ak_ps[mt][s][:].rearrange("p (h k) -> p k h", k=8),
+                out=m[i // 2][:, (i % 2) * 512:(i % 2 + 1) * 512].rearrange("p (k h) -> p k h", k=8),
+                in0=ak_ps[mt][s][:].rearrange("p (h k) -> p k h", k=8),
                 scalar=avg[:, 0:1], in1=ak_sb[mt][:, s * 512:(s + 1) * 512].rearrange("p (k h) -> p k h", k=8),
                 op0=ALU.is_gt, op1=ALU.mult)
 
-        def minmax(i):
-            m_kh = m[i][:].rearrange("p (k h) -> p k h", k=8)
-            nc.vector.tensor_reduce(out=mn[i][:], in_=m_kh, axis=AX.X, op=ALU.min)
-            nc.vector.tensor_reduce(out=mxm[i][:], in_=m_kh, axis=AX.X, op=ALU.max)
+        def minmax(g):
+            m_kh = m[g][:].rearrange("p (k h) -> p k h", h=64)
+            nc.vector.tensor_reduce(out=mn[g][:], in_=m_kh, axis=AX.X, op=ALU.min)
+            nc.vector.tensor_reduce(out=mxm[g][:], in_=m_kh, axis=AX.X, op=ALU.max)
 
-        def small(i):
-            nc.vector.tensor_tensor(out=inv[i][:], in0=mxm[i][:], in1=mn[i][:], op=ALU.subtract)
-            nc.vector.reciprocal(out=inv[i][:], in_=inv[i][:])
+        def small(g):
+            nc.vector.tensor_tensor(out=inv[g][:], in0=mxm[g][:], in1=mn[g][:], op=ALU.subtract)
+            nc.vector.reciprocal(out=inv[g][:], in_=inv[g][:])
 
-        def norm(i, eng, queue):
-            mt, s = pieces[i]
-            m_kh = m[i][:].rearrange("p (k h) -> p k h", k=8)
-            eng.tensor_tensor(out=m_kh, in0=m_kh, in1=mn[i][:].unsqueeze(2).to_broadcast([P, 8, 64]), op=ALU.subtract)
+        def shift(g, eng):
+            m_kh = m[g][:].rearrange("p (k h) -> p k h", h=64)
+            eng.tensor_tensor(out=m_kh, in0=m_kh, in1=mn[g][:].unsqueeze(2).to_broadcast([P, 16, 64]), op=ALU.subtract)
+
+        def scale(i, eng):
             eng.tensor_tensor(out=hat[i][:].rearrange("p (b i k) -> p b k i", i=4, k=8),
-                              in0=m[i][:].rearrange("p (k b i) -> p b k i", k=8, i=4),
-                              in1=inv[i][:].unsqueeze(1).unsqueeze(3).to_broadcast([P, 16, 8, 4]), op=ALU.mult)
-            queue.dma_start(out=hat_v[mt * P:(mt + 1) * P, s * 512:(s + 1) * 512], in_=hat[i][:])
+                              in0=m[i // 2][:, (i % 2) * 512:(i % 2 + 1) * 512].rearrange("p (k b i) -> p b k i", k=8, i=4),
+                              in1=inv[i // 2][:, (i % 2) * 8:(i % 2 + 1) * 8].unsqueeze(1).unsqueeze(3).to_broadcast([P, 16, 8, 4]),
+                              op=ALU.mult)
+
+        def store(i):
+            mt, s = pieces[i]
+            nc.sync.dma_start(out=hat_v[mt * P:(mt + 1) * P, s * 512:(s + 1) * 512], in_=hat[i][:])
 
         select(0)
-        minmax(0)
         select(1)
-        small(0)
-        norm(0, nc.gpsimd, nc.gpsimd)
-        minmax(1)
+        minmax(0)
         select(2)
-        small(1)
-        minmax(2)
-        norm(1, nc.vector, nc.sync)
+        small(0)
+        shift(0, nc.gpsimd)
+        scale(0, nc.gpsimd)
+        scale(1, nc.gpsimd)
         select(3)
-        small(2)
-        minmax(3)
-        norm(2, nc.vector, nc.sync)
-        small(3)
-        norm(3, nc.vector, nc.sync)
+        minmax(1)
+        small(1)
+        shift(1, nc.vector)
+        store(0)
+        store(1)
+        scale(2, nc.vector)
+        store(2)
+        scale(3, nc.vector)
+        store(3)

@@ -138,24 +138,18 @@ def tile_correlationblock_t_kernel(tc, ok, fk, out_0, out_1):
         quant_f(1)
         quant(0)
         ak_passes(0)
-        corr_pass(*jobs[0])
-        corr_pass(*jobs[1])
-        regroup(2, "g")
+        regroup(2, "s")
         regroup(3, "v")
         quant(1)
         ak_passes(1)
-        corr_pass(*jobs[2])
-        corr_pass(*jobs[3])
-        corr_out(*jobs[0])
-        corr_out(*jobs[1])
         quant(3)
         ak_passes(3)
         regroup(4, "s")
         regroup(5, "v")
         quant(2)
         ak_passes(2)
-        corr_pass(*jobs[4])
-        corr_pass(*jobs[5])
+        for i in range(4):
+            corr_pass(*jobs[i])
         quant(5)
         ak_passes(5)
         regroup(6, "s")
@@ -170,11 +164,11 @@ def tile_correlationblock_t_kernel(tc, ok, fk, out_0, out_1):
         ak_out(1, 1, 0, 32, 3)
         quant(6)
         ak_passes(6)
+        corr_out(*jobs[0], eng=nc.vector.tensor_copy)
+        corr_pass(*jobs[4])
+        corr_out(*jobs[1], eng=nc.vector.tensor_copy)
+        corr_pass(*jobs[5])
         corr_out(*jobs[2], eng=nc.vector.tensor_copy)
-        corr_pass(*jobs[6])
-        corr_out(*jobs[3], eng=nc.vector.tensor_copy)
-        corr_pass(*jobs[7])
-        corr_out(*jobs[4], eng=nc.vector.tensor_copy)
         ak_out(0, 1, 32, 64, 4)
         ak_out(1, 1, 32, 64, 5)
 
@@ -182,13 +176,13 @@ def tile_correlationblock_t_kernel(tc, ok, fk, out_0, out_1):
         nc.tensor.matmul(out=mean_ps[:, 0:6], lhsT=ones[:], rhs=rowsum[:], start=True, stop=True)
         nc.vector.tensor_reduce(out=avg[:], in_=mean_ps[:, 0:6], axis=AX.X, op=ALU.add)
 
-        nxt = 8
-        for i in range(5, 16):
+        nxt = 6
+        for i in range(3, 16):
             corr_out(*jobs[i])
             if nxt < 16:
                 corr_pass(*jobs[nxt])
                 nxt += 1
-            if i == 7:
+            if i == 5:
                 corr_pass(*jobs[nxt])
                 nxt += 1
 
@@ -243,8 +237,8 @@ def tile_correlationblock_t_kernel(tc, ok, fk, out_0, out_1):
         small(1)
         shift(1, nc.vector)
         store(0)
-        store(1)
         scale(2, nc.vector)
         store(2)
+        store(1)
         scale(3, nc.vector)
         store(3)

@@ -18,7 +18,6 @@ PACK = 4
 CH = 512
 NCH = 8
 
-FK_UNITS = (512, 512, 512, 512)
 OK_UNITS = (1024, 1024, 1024, 512, 512)
 
 
@@ -48,11 +47,16 @@ def tile_correlationblock_t_kernel(tc, ok, fk, out_0, out_1):
             for i in range(units[u] // step):
                 table[lo // step + i] = t[:, :, i * step:(i + 1) * step]
 
-        load(fk_v, FK_UNITS, 0, fk_at, 512, "fk_raw")
-        load(fk_v, FK_UNITS, 1, fk_at, 512, "fk_raw")
-        load(fk_v, FK_UNITS, 2, fk_at, 512, "fk_raw")
+        def load_fk(q):
+            t = keep.tile([P, 2, 1024], BF16, name="fk_raw%d" % q)
+            nc.sync.dma_start(out=t[:], in_=fk_v[:, 2 * (q % 2):2 * (q % 2) + 2, (q // 2) * 1024:(q // 2 + 1) * 1024])
+            fk_at[q] = t
+
+        load_fk(0)
+        load_fk(1)
+        load_fk(2)
         load(ok_v, OK_UNITS, 0, ok_at, CH, "ok_raw")
-        load(fk_v, FK_UNITS, 3, fk_at, 512, "fk_raw")
+        load_fk(3)
         for u in range(1, 5):
             load(ok_v, OK_UNITS, u, ok_at, CH, "ok_raw")
 
@@ -71,8 +75,8 @@ def tile_correlationblock_t_kernel(tc, ok, fk, out_0, out_1):
         def fsum(q):
             with nc.allow_low_precision(reason="float32 sum, rounded once to bfloat16 as the task says"):
                 nc.vector.tensor_reduce(
-                    out=fgrp[:, q * 64:(q + 1) * 64, :].rearrange("p g j -> p j g"),
-                    in_=fk_at[q].rearrange("p j (g d) -> p j g d", d=8), axis=AX.X, op=ALU.add)
+                    out=fgrp[:, (q // 2) * P:(q // 2 + 1) * P, 2 * (q % 2):2 * (q % 2) + 2].rearrange("p g j -> p j g"),
+                    in_=fk_at[q][:].rearrange("p j (g d) -> p j g d", d=8), axis=AX.X, op=ALU.add)
 
         def quant_f(mt):
             nc.vector.quantize_mx(
@@ -126,7 +130,7 @@ def tile_correlationblock_t_kernel(tc, ok, fk, out_0, out_1):
                 nc.sync.dma_start(out=corr_v[mt * P:(mt + 1) * P, (c - 1) * CH:(c + 1) * CH],
                                   in_=corr_sb[mt][:, (c - 1) * CH:(c + 1) * CH])
 
-        jobs = [(c, mt) for c in range(NCH) for mt in range(2)]
+        jobs = [(c, mt) for cp in range(NCH // 2) for mt in range(2) for c in (2 * cp, 2 * cp + 1)]
 
         fsum(0)
         fsum(1)

@@ -137,8 +137,8 @@ def tile_correlationblock_t_kernel(tc, ok, fk, out_0, out_1):
         fsum(2)
         regroup(0, "s")
         regroup(1, "g")
-        quant_f(0)
         fsum(3)
+        quant_f(0)
         quant_f(1)
         quant(0)
         ak_passes(0)
@@ -210,19 +210,34 @@ def tile_correlationblock_t_kernel(tc, ok, fk, out_0, out_1):
             nc.vector.tensor_reduce(out=mn[g][:], in_=m_kh, axis=AX.X, op=ALU.min)
             nc.vector.tensor_reduce(out=mxm[g][:], in_=m_kh, axis=AX.X, op=ALU.max)
 
-        def small(g):
+        nq = keep.tile([P, 8], F32)
+
+        def spread(g):
             nc.vector.tensor_tensor(out=inv[g][:], in0=mxm[g][:], in1=mn[g][:], op=ALU.subtract)
+
+        def recip(g):
             nc.vector.reciprocal(out=inv[g][:], in_=inv[g][:])
 
-        def shift(g, eng):
-            m_kh = m[g][:].rearrange("p (k h) -> p k h", h=64)
-            eng.tensor_tensor(out=m_kh, in0=m_kh, in1=mn[g][:].unsqueeze(2).to_broadcast([P, 16, 64]), op=ALU.subtract)
+        def shift(i0, i1):
+            g = i0 // 2
+            lo, hi = (i0 % 2) * 8, (i0 % 2) * 8 + (i1 - i0) * 8
+            m_kh = m[g][:, lo * 64:hi * 64].rearrange("p (k h) -> p k h", h=64)
+            nc.vector.tensor_tensor(out=m_kh, in0=m_kh, in1=mn[g][:, lo:hi].unsqueeze(2).to_broadcast([P, hi - lo, 64]),
+                                    op=ALU.subtract)
 
-        def scale(i, eng):
-            eng.tensor_tensor(out=hat[i][:].rearrange("p (b i k) -> p b k i", i=4, k=8),
-                              in0=m[i // 2][:, (i % 2) * 512:(i % 2 + 1) * 512].rearrange("p (k b i) -> p b k i", k=8, i=4),
-                              in1=inv[i // 2][:, (i % 2) * 8:(i % 2 + 1) * 8].unsqueeze(1).unsqueeze(3).to_broadcast([P, 16, 8, 4]),
-                              op=ALU.mult)
+        def scale(i):
+            nc.vector.tensor_tensor(out=hat[i][:].rearrange("p (b i k) -> p b k i", i=4, k=8),
+                                    in0=m[i // 2][:, (i % 2) * 512:(i % 2 + 1) * 512].rearrange("p (k b i) -> p b k i", k=8, i=4),
+                                    in1=inv[i // 2][:, (i % 2) * 8:(i % 2 + 1) * 8].unsqueeze(1).unsqueeze(3).to_broadcast([P, 16, 8, 4]),
+                                    op=ALU.mult)
+
+        def piece0_gpsimd():
+            nc.gpsimd.tensor_tensor(out=nq[:], in0=mn[0][:, 0:8], in1=inv[0][:, 0:8], op=ALU.mult)
+            m_kh = m[0][:, 0:512].rearrange("p (k h) -> p k h", h=64)
+            nc.gpsimd.tensor_tensor(out=m_kh, in0=m_kh, in1=inv[0][:, 0:8].unsqueeze(2).to_broadcast([P, 8, 64]), op=ALU.mult)
+            nc.gpsimd.tensor_tensor(out=hat[0][:].rearrange("p (b i k) -> p b k i", i=4, k=8),
+                                    in0=m[0][:, 0:512].rearrange("p (k b i) -> p b k i", k=8, i=4),
+                                    in1=nq[:].unsqueeze(1).unsqueeze(3).to_broadcast([P, 16, 8, 4]), op=ALU.subtract)
 
         def store(i):
             mt, s = pieces[i]
@@ -231,18 +246,20 @@ def tile_correlationblock_t_kernel(tc, ok, fk, out_0, out_1):
         select(0)
         select(1)
         minmax(0)
+        spread(0)
+        recip(0)
+        piece0_gpsimd()
         select(2)
-        small(0)
-        shift(0, nc.gpsimd)
-        scale(0, nc.gpsimd)
-        scale(1, nc.gpsimd)
         select(3)
         minmax(1)
-        small(1)
-        shift(1, nc.vector)
+        spread(1)
+        shift(1, 2)
+        recip(1)
+        shift(2, 4)
         store(0)
-        scale(2, nc.vector)
-        store(2)
+        scale(1)
         store(1)
-        scale(3, nc.vector)
+        scale(2)
+        store(2)
+        scale(3)
         store(3)

@@ -19,6 +19,7 @@ CH = 512
 NCH = 8
 
 OK_UNITS = (1024, 1024, 1024, 512, 512)
+FK_PIECES = ((0, 0, 1), (0, 1, 1), (0, 2, 2), (1, 0, 2), (1, 2, 2))
 
 
 def tile_correlationblock_t_kernel(tc, ok, fk, out_0, out_1):
@@ -48,15 +49,15 @@ def tile_correlationblock_t_kernel(tc, ok, fk, out_0, out_1):
                 table[lo // step + i] = t[:, :, i * step:(i + 1) * step]
 
         def load_fk(q):
-            t = keep.tile([P, 2, 1024], BF16, name="fk_raw%d" % q)
-            nc.sync.dma_start(out=t[:], in_=fk_v[:, 2 * (q % 2):2 * (q % 2) + 2, (q // 2) * 1024:(q // 2 + 1) * 1024])
+            mt, j0, nj = FK_PIECES[q]
+            t = keep.tile([P, nj, 1024], BF16, name="fk_raw%d" % q)
+            nc.sync.dma_start(out=t[:], in_=fk_v[:, j0:j0 + nj, mt * 1024:(mt + 1) * 1024])
             fk_at[q] = t
 
-        load_fk(0)
-        load_fk(1)
-        load_fk(2)
+        for q in range(4):
+            load_fk(q)
         load(ok_v, OK_UNITS, 0, ok_at, CH, "ok_raw")
-        load_fk(3)
+        load_fk(4)
         for u in range(1, 5):
             load(ok_v, OK_UNITS, u, ok_at, CH, "ok_raw")
 
@@ -73,15 +74,14 @@ def tile_correlationblock_t_kernel(tc, ok, fk, out_0, out_1):
         avg = keep.tile([P, 1], F32)
 
         def fsum(q):
+            mt, j0, nj = FK_PIECES[q]
             with nc.allow_low_precision(reason="float32 sum, rounded once to bfloat16 as the task says"):
                 nc.vector.tensor_reduce(
-                    out=fgrp[:, (q // 2) * P:(q // 2 + 1) * P, 2 * (q % 2):2 * (q % 2) + 2].rearrange("p g j -> p j g"),
+                    out=fgrp[:, mt * P:(mt + 1) * P, j0:j0 + nj].rearrange("p g j -> p j g"),
                     in_=fk_at[q][:].rearrange("p j (g d) -> p j g d", d=8), axis=AX.X, op=ALU.add)
 
-        def quant_f(mt):
-            nc.vector.quantize_mx(
-                out=f_codes[:, mt * P:(mt + 1) * P].bitcast(FP8X4), scales=f_scales[:, mt * P:(mt + 1) * P],
-                in_=fgrp[:, mt * P:(mt + 1) * P, :].rearrange("p g j -> p (g j)"))
+        def quant_f():
+            nc.vector.quantize_mx(out=f_codes[:].bitcast(FP8X4), scales=f_scales[:], in_=fgrp[:].rearrange("p g j -> p (g j)"))
 
         def regroup(c, eng):
             src = ok_at[c].rearrange("p j (h w k) -> p w h j k", w=4, k=8)
@@ -132,14 +132,12 @@ def tile_correlationblock_t_kernel(tc, ok, fk, out_0, out_1):
 
         jobs = [(c, mt) for cp in range(NCH // 2) for mt in range(2) for c in (2 * cp, 2 * cp + 1)]
 
-        fsum(0)
-        fsum(1)
-        fsum(2)
+        for q in range(4):
+            fsum(q)
         regroup(0, "s")
         regroup(1, "g")
-        fsum(3)
-        quant_f(0)
-        quant_f(1)
+        fsum(4)
+        quant_f()
         quant(0)
         ak_passes(0)
         regroup(2, "s")
@@ -191,53 +189,51 @@ def tile_correlationblock_t_kernel(tc, ok, fk, out_0, out_1):
                 nxt += 1
 
         pieces = [(0, 0), (1, 0), (0, 1), (1, 1)]
-        m = [keep.tile([P, 1024], F32, name="m%d" % i) for i in range(2)]
+        m = keep.tile([P, 2048], F32)
         hat = [keep.tile([P, 512], F32, name="hat%d" % i) for i in range(4)]
-        mn = [keep.tile([P, 16], F32, name="mn%d" % i) for i in range(2)]
-        mxm = [keep.tile([P, 16], F32, name="mxm%d" % i) for i in range(2)]
-        inv = [keep.tile([P, 16], F32, name="inv%d" % i) for i in range(2)]
+        mn = keep.tile([P, 32], F32)
+        mxm = keep.tile([P, 32], F32)
+        inv = keep.tile([P, 32], F32)
+        q0 = keep.tile([P, 8], F32)
 
         def select(i):
             mt, s = pieces[i]
             nc.vector.scalar_tensor_tensor(
-                out=m[i // 2][:, (i % 2) * 512:(i % 2 + 1) * 512].rearrange("p (k h) -> p k h", k=8),
+                out=m[:, i * 512:(i + 1) * 512].rearrange("p (k h) -> p k h", k=8),
                 in0=ak_ps[mt][s][:].rearrange("p (h k) -> p k h", k=8),
                 scalar=avg[:, 0:1], in1=ak_sb[mt][:, s * 512:(s + 1) * 512].rearrange("p (k h) -> p k h", k=8),
                 op0=ALU.is_gt, op1=ALU.mult)
 
         def minmax(g):
-            m_kh = m[g][:].rearrange("p (k h) -> p k h", h=64)
-            nc.vector.tensor_reduce(out=mn[g][:], in_=m_kh, axis=AX.X, op=ALU.min)
-            nc.vector.tensor_reduce(out=mxm[g][:], in_=m_kh, axis=AX.X, op=ALU.max)
-
-        nq = keep.tile([P, 8], F32)
+            m_kh = m[:, g * 1024:(g + 1) * 1024].rearrange("p (k h) -> p k h", h=64)
+            nc.vector.tensor_reduce(out=mn[:, g * 16:(g + 1) * 16], in_=m_kh, axis=AX.X, op=ALU.min)
+            nc.vector.tensor_reduce(out=mxm[:, g * 16:(g + 1) * 16], in_=m_kh, axis=AX.X, op=ALU.max)
 
         def spread(g):
-            nc.vector.tensor_tensor(out=inv[g][:], in0=mxm[g][:], in1=mn[g][:], op=ALU.subtract)
+            nc.vector.tensor_tensor(out=inv[:, g * 16:(g + 1) * 16], in0=mxm[:, g * 16:(g + 1) * 16],
+                                    in1=mn[:, g * 16:(g + 1) * 16], op=ALU.subtract)
 
         def recip(g):
-            nc.vector.reciprocal(out=inv[g][:], in_=inv[g][:])
+            nc.vector.reciprocal(out=inv[:, g * 16:(g + 1) * 16], in_=inv[:, g * 16:(g + 1) * 16])
 
         def shift(i0, i1):
-            g = i0 // 2
-            lo, hi = (i0 % 2) * 8, (i0 % 2) * 8 + (i1 - i0) * 8
-            m_kh = m[g][:, lo * 64:hi * 64].rearrange("p (k h) -> p k h", h=64)
-            nc.vector.tensor_tensor(out=m_kh, in0=m_kh, in1=mn[g][:, lo:hi].unsqueeze(2).to_broadcast([P, hi - lo, 64]),
+            m_kh = m[:, i0 * 512:i1 * 512].rearrange("p (k h) -> p k h", h=64)
+            nc.vector.tensor_tensor(out=m_kh, in0=m_kh, in1=mn[:, i0 * 8:i1 * 8].unsqueeze(2).to_broadcast([P, (i1 - i0) * 8, 64]),
                                     op=ALU.subtract)
 
         def scale(i):
             nc.vector.tensor_tensor(out=hat[i][:].rearrange("p (b i k) -> p b k i", i=4, k=8),
-                                    in0=m[i // 2][:, (i % 2) * 512:(i % 2 + 1) * 512].rearrange("p (k b i) -> p b k i", k=8, i=4),
-                                    in1=inv[i // 2][:, (i % 2) * 8:(i % 2 + 1) * 8].unsqueeze(1).unsqueeze(3).to_broadcast([P, 16, 8, 4]),
+                                    in0=m[:, i * 512:(i + 1) * 512].rearrange("p (k b i) -> p b k i", k=8, i=4),
+                                    in1=inv[:, i * 8:(i + 1) * 8].unsqueeze(1).unsqueeze(3).to_broadcast([P, 16, 8, 4]),
                                     op=ALU.mult)
 
         def piece0_gpsimd():
-            nc.gpsimd.tensor_tensor(out=nq[:], in0=mn[0][:, 0:8], in1=inv[0][:, 0:8], op=ALU.mult)
-            m_kh = m[0][:, 0:512].rearrange("p (k h) -> p k h", h=64)
-            nc.gpsimd.tensor_tensor(out=m_kh, in0=m_kh, in1=inv[0][:, 0:8].unsqueeze(2).to_broadcast([P, 8, 64]), op=ALU.mult)
+            nc.gpsimd.tensor_tensor(out=q0[:], in0=mn[:, 0:8], in1=inv[:, 0:8], op=ALU.mult)
+            m_kh = m[:, 0:512].rearrange("p (k h) -> p k h", h=64)
+            nc.gpsimd.tensor_tensor(out=m_kh, in0=m_kh, in1=inv[:, 0:8].unsqueeze(2).to_broadcast([P, 8, 64]), op=ALU.mult)
             nc.gpsimd.tensor_tensor(out=hat[0][:].rearrange("p (b i k) -> p b k i", i=4, k=8),
-                                    in0=m[0][:, 0:512].rearrange("p (k b i) -> p b k i", k=8, i=4),
-                                    in1=nq[:].unsqueeze(1).unsqueeze(3).to_broadcast([P, 16, 8, 4]), op=ALU.subtract)
+                                    in0=m[:, 0:512].rearrange("p (k b i) -> p b k i", k=8, i=4),
+                                    in1=q0[:].unsqueeze(1).unsqueeze(3).to_broadcast([P, 16, 8, 4]), op=ALU.subtract)
 
         def store(i):
             mt, s = pieces[i]
@@ -253,9 +249,8 @@ def tile_correlationblock_t_kernel(tc, ok, fk, out_0, out_1):
         select(3)
         minmax(1)
         spread(1)
-        shift(1, 2)
+        shift(1, 4)
         recip(1)
-        shift(2, 4)
         store(0)
         scale(1)
         store(1)

@@ -216,16 +216,14 @@ def tile_correlationblock_t_kernel(tc, ok, fk, out_0, out_1):
         def recip(g):
             nc.vector.reciprocal(out=inv[:, g * 16:(g + 1) * 16], in_=inv[:, g * 16:(g + 1) * 16])
 
-        def shift(i0, i1):
-            m_kh = m[:, i0 * 512:i1 * 512].rearrange("p (k h) -> p k h", h=64)
-            nc.vector.tensor_tensor(out=m_kh, in0=m_kh, in1=mn[:, i0 * 8:i1 * 8].unsqueeze(2).to_broadcast([P, (i1 - i0) * 8, 64]),
-                                    op=ALU.subtract)
+        def normalise(i):
+            for c in range(i * 8, (i + 1) * 8):
+                run = m[:, c * 64:(c + 1) * 64]
+                nc.vector.tensor_scalar(out=run, in0=run, scalar1=mn[:, c:c + 1], scalar2=inv[:, c:c + 1], op0=ALU.subtract, op1=ALU.mult)
 
-        def scale(i):
-            nc.vector.tensor_tensor(out=hat[i][:].rearrange("p (b i k) -> p b k i", i=4, k=8),
-                                    in0=m[:, i * 512:(i + 1) * 512].rearrange("p (k b i) -> p b k i", k=8, i=4),
-                                    in1=inv[:, i * 8:(i + 1) * 8].unsqueeze(1).unsqueeze(3).to_broadcast([P, 16, 8, 4]),
-                                    op=ALU.mult)
+        def reorder(i):
+            nc.scalar.copy(out=hat[i][:].rearrange("p (b i k) -> p b k i", i=4, k=8),
+                           in_=m[:, i * 512:(i + 1) * 512].rearrange("p (k b i) -> p b k i", k=8, i=4))
 
         def piece0_gpsimd():
             nc.gpsimd.tensor_tensor(out=q0[:], in0=mn[:, 0:8], in1=inv[:, 0:8], op=ALU.mult)
@@ -249,12 +247,9 @@ def tile_correlationblock_t_kernel(tc, ok, fk, out_0, out_1):
         select(3)
         minmax(1)
         spread(1)
-        shift(1, 4)
         recip(1)
         store(0)
-        scale(1)
-        store(1)
-        scale(2)
-        store(2)
-        scale(3)
-        store(3)
+        for i in range(1, 4):
+            normalise(i)
+            reorder(i)
+            store(i)

@@ -18,7 +18,8 @@ PACK = 4
 CH = 512
 NCH = 8
 
-OK_UNITS = (1024, 1024, 1024, 512, 512)
+OK_UNITS = (512, 1024, 1024, 1024, 512)
+VF = 64
 FK_PIECES = ((0, 0, 1), (0, 1, 1), (0, 2, 2), (1, 0, 2), (1, 2, 2))
 
 
@@ -58,10 +59,12 @@ def tile_correlationblock_t_kernel(tc, ok, fk, out_0, out_1):
             load_fk(q)
         load(ok_v, OK_UNITS, 0, ok_at, CH, "ok_raw")
         load_fk(4)
-        for u in range(1, 5):
+        for u in range(1, len(OK_UNITS)):
             load(ok_v, OK_UNITS, u, ok_at, CH, "ok_raw")
 
         fgrp = keep.tile([P, 256, PACK], BF16, align_bytes=64)
+        half_sum = keep.tile([P, PACK, P - VF, 4], F32)
+        quarter_sum = keep.tile([P, PACK, P - VF, 2], F32)
         f_codes = keep.tile([P, 256], U32, align_bytes=64)
         f_scales = keep.tile([P, 256], U8, align_bytes=64)
         o_codes = keep.tile([P, NCH * CH], U32, align_bytes=64)
@@ -75,24 +78,34 @@ def tile_correlationblock_t_kernel(tc, ok, fk, out_0, out_1):
 
         def fsum(q):
             mt, j0, nj = FK_PIECES[q]
+            ng = VF if mt == 0 else P
             with nc.allow_low_precision(reason="float32 sum, rounded once to bfloat16 as the task says"):
                 nc.vector.tensor_reduce(
-                    out=fgrp[:, mt * P:(mt + 1) * P, j0:j0 + nj].rearrange("p g j -> p j g"),
-                    in_=fk_at[q][:].rearrange("p j (g d) -> p j g d", d=8), axis=AX.X, op=ALU.add)
+                    out=fgrp[:, mt * P:mt * P + ng, j0:j0 + nj].rearrange("p g j -> p j g"),
+                    in_=fk_at[q][:, :, 0:ng * 8].rearrange("p j (g d) -> p j g d", d=8), axis=AX.X, op=ALU.add)
+
+        def fsum_gpsimd_first(q):
+            mt, j0, nj = FK_PIECES[q]
+            src = fk_at[q][:, :, VF * 8:1024].rearrange("p j (g d) -> p j g d", d=8)
+            nc.gpsimd.tensor_tensor(out=half_sum[:, j0:j0 + nj], in0=src[:, :, :, 0:4], in1=src[:, :, :, 4:8], op=ALU.add)
+
+        def fsum_gpsimd_rest():
+            nc.gpsimd.tensor_tensor(out=quarter_sum[:], in0=half_sum[:, :, :, 0:2], in1=half_sum[:, :, :, 2:4], op=ALU.add)
+            with nc.allow_low_precision(reason="float32 sum, rounded once to bfloat16 as the task says"):
+                nc.gpsimd.tensor_tensor(out=fgrp[:, VF:P, :].rearrange("p g j -> p j g"),
+                                        in0=quarter_sum[:, :, :, 0], in1=quarter_sum[:, :, :, 1], op=ALU.add)
 
         def quant_f():
             nc.vector.quantize_mx(out=f_codes[:].bitcast(FP8X4), scales=f_scales[:], in_=fgrp[:].rearrange("p g j -> p (g j)"))
 
-        def regroup(c, eng):
-            src = ok_at[c].rearrange("p j (h w k) -> p w h j k", w=4, k=8)
-            dst = grp[c][:].rearrange("p (w h k) j -> p w h j k", w=4, k=8)
+        def regroup(c, eng, w0=0, w1=4):
+            src = ok_at[c].rearrange("p j (h w k) -> p w h j k", w=4, k=8)[:, w0:w1]
+            dst = grp[c][:].rearrange("p (w h k) j -> p w h j k", w=4, k=8)[:, w0:w1]
             if eng == "v":
                 nc.vector.tensor_copy(out=dst, in_=src)
-            for w in range(4):
-                if eng == "s":
+            else:
+                for w in range(w1 - w0):
                     nc.scalar.copy(out=dst[:, w], in_=src[:, w])
-                if eng == "g":
-                    nc.gpsimd.tensor_scalar(out=dst[:, w], in0=src[:, w], scalar1=1.0, scalar2=0.0, op0=ALU.mult, op1=ALU.add)
 
         def quant(c):
             nc.vector.quantize_mx(
@@ -132,40 +145,43 @@ def tile_correlationblock_t_kernel(tc, ok, fk, out_0, out_1):
 
         jobs = [(c, mt) for cp in range(NCH // 2) for mt in range(2) for c in (2 * cp, 2 * cp + 1)]
 
-        for q in range(4):
+        for q in range(3):
+            fsum_gpsimd_first(q)
+        fsum_gpsimd_rest()
+        for q in range(5):
             fsum(q)
         regroup(0, "s")
-        regroup(1, "g")
-        fsum(4)
         quant_f()
         quant(0)
         ak_passes(0)
-        regroup(2, "s")
-        regroup(3, "v")
+        regroup(1, "s")
+        regroup(2, "v")
         quant(1)
         ak_passes(1)
-        quant(3)
-        ak_passes(3)
-        regroup(4, "s")
-        regroup(5, "v")
         quant(2)
         ak_passes(2)
-        for i in range(4):
-            corr_pass(*jobs[i])
-        quant(5)
-        ak_passes(5)
-        regroup(6, "s")
-        regroup(7, "v")
+        regroup(4, "s")
+        regroup(3, "v")
         quant(4)
         ak_passes(4)
-        quant(7)
-        ak_passes(7)
+        quant(3)
+        ak_passes(3)
+        for i in range(4):
+            corr_pass(*jobs[i])
+        regroup(6, "s")
+        regroup(7, "s", 0, 2)
         ak_out(0, 0, 0, 64, 0)
         ak_out(1, 0, 0, 64, 1)
+        regroup(5, "v")
+        regroup(7, "v", 2, 4)
+        quant(5)
+        ak_passes(5)
         ak_out(0, 1, 0, 32, 2)
         ak_out(1, 1, 0, 32, 3)
         quant(6)
         ak_passes(6)
+        quant(7)
+        ak_passes(7)
         corr_out(*jobs[0], eng=nc.vector.tensor_copy)
         corr_pass(*jobs[4])
         corr_out(*jobs[1], eng=nc.vector.tensor_copy)

@@ -210,7 +210,7 @@ def tile_correlationblock_t_kernel(tc, ok, fk, out_0, out_1):
         mn = keep.tile([P, 32], F32)
         mxm = keep.tile([P, 32], F32)
         inv = keep.tile([P, 32], F32)
-        q0 = keep.tile([P, 8], F32)
+        mask = keep.tile([P, 512], F32)
 
         def select(i):
             mt, s = pieces[i]
@@ -220,10 +220,15 @@ def tile_correlationblock_t_kernel(tc, ok, fk, out_0, out_1):
                 scalar=avg[:, 0:1], in1=ak_sb[mt][:, s * 512:(s + 1) * 512].rearrange("p (k h) -> p k h", k=8),
                 op0=ALU.is_gt, op1=ALU.mult)
 
-        def minmax(g):
-            m_kh = m[:, g * 1024:(g + 1) * 1024].rearrange("p (k h) -> p k h", h=64)
-            nc.vector.tensor_reduce(out=mn[:, g * 16:(g + 1) * 16], in_=m_kh, axis=AX.X, op=ALU.min)
-            nc.vector.tensor_reduce(out=mxm[:, g * 16:(g + 1) * 16], in_=m_kh, axis=AX.X, op=ALU.max)
+        def select_gpsimd(i):
+            mt, s = pieces[i]
+            ak = ak_sb[mt][:, s * 512:(s + 1) * 512]
+            nc.gpsimd.tensor_scalar(out=mask[:], in0=ak, scalar1=avg[:, 0:1], scalar2=1.0, op0=ALU.is_gt, op1=ALU.mult)
+            nc.gpsimd.tensor_tensor(out=m[:, i * 512:(i + 1) * 512], in0=mask[:], in1=ak, op=ALU.mult)
+
+        def extreme(out, op, i0, i1):
+            nc.vector.tensor_reduce(out=out[:, i0 * 8:i1 * 8], in_=m[:, i0 * 512:i1 * 512].rearrange("p (k h) -> p k h", h=64),
+                                    axis=AX.X, op=op)
 
         def spread(g):
             nc.vector.tensor_tensor(out=inv[:, g * 16:(g + 1) * 16], in0=mxm[:, g * 16:(g + 1) * 16],
@@ -241,31 +246,31 @@ def tile_correlationblock_t_kernel(tc, ok, fk, out_0, out_1):
             nc.scalar.copy(out=hat[i][:].rearrange("p (b i k) -> p b k i", i=4, k=8),
                            in_=m[:, i * 512:(i + 1) * 512].rearrange("p (k b i) -> p b k i", k=8, i=4))
 
-        def piece0_gpsimd():
-            nc.gpsimd.tensor_tensor(out=q0[:], in0=mn[:, 0:8], in1=inv[:, 0:8], op=ALU.mult)
-            m_kh = m[:, 0:512].rearrange("p (k h) -> p k h", h=64)
-            nc.gpsimd.tensor_tensor(out=m_kh, in0=m_kh, in1=inv[:, 0:8].unsqueeze(2).to_broadcast([P, 8, 64]), op=ALU.mult)
-            nc.gpsimd.tensor_tensor(out=hat[0][:].rearrange("p (b i k) -> p b k i", i=4, k=8),
-                                    in0=m[:, 0:512].rearrange("p (k b i) -> p b k i", k=8, i=4),
-                                    in1=q0[:].unsqueeze(1).unsqueeze(3).to_broadcast([P, 16, 8, 4]), op=ALU.subtract)
-
         def store(i):
             mt, s = pieces[i]
             nc.sync.dma_start(out=hat_v[mt * P:(mt + 1) * P, s * 512:(s + 1) * 512], in_=hat[i][:])
 
         select(0)
+        select_gpsimd(3)
         select(1)
-        minmax(0)
-        spread(0)
-        recip(0)
-        piece0_gpsimd()
         select(2)
-        select(3)
-        minmax(1)
+        extreme(mn, ALU.min, 0, 1)
+        extreme(mn, ALU.min, 1, 2)
+        extreme(mxm, ALU.max, 0, 2)
+        extreme(mn, ALU.min, 2, 3)
+        spread(0)
+        extreme(mxm, ALU.max, 2, 3)
+        recip(0)
+        extreme(mn, ALU.min, 3, 4)
+        normalise(0)
+        extreme(mxm, ALU.max, 3, 4)
+        normalise(1)
         spread(1)
+        for i in range(2):
+            reorder(i)
+            store(i)
         recip(1)
-        store(0)
-        for i in range(1, 4):
+        for i in range(2, 4):
             normalise(i)
             reorder(i)
             store(i)

@@ -73,7 +73,7 @@ def tile_correlationblock_t_kernel(tc, ok, fk, out_0, out_1):
         corr_sb = [keep.tile([P, NCH * CH], F32, name="corr_sb%d" % mt) for mt in range(2)]
         ak_sb = [keep.tile([P, 1024], F32, name="ak_sb%d" % mt) for mt in range(2)]
         ak_ps = [[ps_ak.tile([P, 512], F32, name="ak_ps%d%d" % (mt, s)) for s in range(2)] for mt in range(2)]
-        rowsum = keep.tile([P, 6], F32)
+        rowsum = keep.tile([P, 4], F32)
         avg = keep.tile([P, 1], F32)
 
         def fsum(q):
@@ -122,10 +122,16 @@ def tile_correlationblock_t_kernel(tc, ok, fk, out_0, out_1):
                 for w in range(4):
                     mx(ak_ps[mt][c // 4][:, (c % 4) * P:(c % 4 + 1) * P], mt, c * CH + w * P, P, w == 0, w == 3)
 
-        def ak_out(mt, s, h0, h1, col):
+        def ak_out(mt, s, col):
             nc.scalar.activation(
-                out=ak_sb[mt][:, s * 512:(s + 1) * 512].rearrange("p (k h) -> p k h", k=8)[:, :, h0:h1],
-                in_=ak_ps[mt][s][:].rearrange("p (h k) -> p k h", k=8)[:, :, h0:h1], func=ACT.Copy,
+                out=ak_sb[mt][:, s * 512:(s + 1) * 512].rearrange("p (k h) -> p k h", k=8),
+                in_=ak_ps[mt][s][:].rearrange("p (h k) -> p k h", k=8), func=ACT.Copy,
+                accum_out=rowsum[:, col:col + 1])
+
+        def ak_out_vector(mt, s, col):
+            nc.vector.tensor_scalar(
+                out=ak_sb[mt][:, s * 512:(s + 1) * 512].rearrange("p (k h) -> p k h", k=8),
+                in0=ak_ps[mt][s][:].rearrange("p (h k) -> p k h", k=8), scalar1=1.0, scalar2=0.0, op0=ALU.mult, op1=ALU.add,
                 accum_out=rowsum[:, col:col + 1])
 
         banks = {}
@@ -170,39 +176,34 @@ def tile_correlationblock_t_kernel(tc, ok, fk, out_0, out_1):
             corr_pass(*jobs[i])
         regroup(6, "s")
         regroup(7, "s", 0, 2)
-        ak_out(0, 0, 0, 64, 0)
-        ak_out(1, 0, 0, 64, 1)
+        corr_out(*jobs[0])
+        corr_out(*jobs[1])
+        ak_out(0, 0, 0)
+        ak_out(1, 0, 1)
         regroup(5, "v")
         regroup(7, "v", 2, 4)
         quant(5)
         ak_passes(5)
-        ak_out(0, 1, 0, 32, 2)
-        ak_out(1, 1, 0, 32, 3)
         quant(6)
         ak_passes(6)
         quant(7)
         ak_passes(7)
-        corr_out(*jobs[0], eng=nc.vector.tensor_copy)
         corr_pass(*jobs[4])
-        corr_out(*jobs[1], eng=nc.vector.tensor_copy)
         corr_pass(*jobs[5])
         corr_out(*jobs[2], eng=nc.vector.tensor_copy)
-        ak_out(0, 1, 32, 64, 4)
-        ak_out(1, 1, 32, 64, 5)
+        ak_out(0, 1, 2)
+        ak_out_vector(1, 1, 3)
+        corr_out(*jobs[3], eng=nc.vector.tensor_copy)
 
         mean_ps = ps_c.tile([P, CH], F32, name="acc")
-        nc.tensor.matmul(out=mean_ps[:, 0:6], lhsT=ones[:], rhs=rowsum[:], start=True, stop=True)
-        nc.vector.tensor_reduce(out=avg[:], in_=mean_ps[:, 0:6], axis=AX.X, op=ALU.add)
+        nc.tensor.matmul(out=mean_ps[:, 0:4], lhsT=ones[:], rhs=rowsum[:], start=True, stop=True)
+        nc.vector.tensor_reduce(out=avg[:], in_=mean_ps[:, 0:4], axis=AX.X, op=ALU.add)
 
-        nxt = 6
-        for i in range(3, 16):
+        corr_pass(*jobs[6])
+        for i in range(4, 16):
             corr_out(*jobs[i])
-            if nxt < 16:
-                corr_pass(*jobs[nxt])
-                nxt += 1
-            if i == 5:
-                corr_pass(*jobs[nxt])
-                nxt += 1
+            if i + 3 < 16:
+                corr_pass(*jobs[i + 3])
 
         pieces = [(0, 0), (1, 0), (0, 1), (1, 1)]
         m = keep.tile([P, 2048], F32)
@@ -242,9 +243,9 @@ def tile_correlationblock_t_kernel(tc, ok, fk, out_0, out_1):
                 run = m[:, c * 64:(c + 1) * 64]
                 nc.vector.tensor_scalar(out=run, in0=run, scalar1=mn[:, c:c + 1], scalar2=inv[:, c:c + 1], op0=ALU.subtract, op1=ALU.mult)
 
-        def reorder(i):
-            nc.scalar.copy(out=hat[i][:].rearrange("p (b i k) -> p b k i", i=4, k=8),
-                           in_=m[:, i * 512:(i + 1) * 512].rearrange("p (k b i) -> p b k i", k=8, i=4))
+        def reorder(i, copy):
+            copy(out=hat[i][:].rearrange("p (b i k) -> p b k i", i=4, k=8),
+                 in_=m[:, i * 512:(i + 1) * 512].rearrange("p (k b i) -> p b k i", k=8, i=4))
 
         def store(i):
             mt, s = pieces[i]
@@ -267,10 +268,12 @@ def tile_correlationblock_t_kernel(tc, ok, fk, out_0, out_1):
         normalise(1)
         spread(1)
         for i in range(2):
-            reorder(i)
+            reorder(i, nc.scalar.copy)
             store(i)
         recip(1)
-        for i in range(2, 4):
-            normalise(i)
-            reorder(i)
-            store(i)
+        normalise(2)
+        reorder(2, nc.scalar.copy)
+        store(2)
+        normalise(3)
+        reorder(3, nc.vector.tensor_copy)
+        store(3)

@@ -1,6 +1,7 @@
 from contextlib import ExitStack
 
 import concourse.mybir as mybir
+from concourse.masks import make_identity
 
 FLOPS = 2 * 512 * 256 * 4096
 
@@ -38,6 +39,8 @@ def tile_correlationblock_t_kernel(tc, ok, fk, out_0, out_1):
 
         ones = keep.tile([P, P], F32)
         nc.vector.memset(ones[:], 1.0 / 262144.0)
+        ident = keep.tile([P, P], BF16)
+        make_identity(nc, ident[:])
 
         fk_at = {}
         ok_at = {}
@@ -63,8 +66,6 @@ def tile_correlationblock_t_kernel(tc, ok, fk, out_0, out_1):
             load(ok_v, OK_UNITS, u, ok_at, CH, "ok_raw")
 
         fgrp = keep.tile([P, 256, PACK], BF16, align_bytes=64)
-        half_sum = keep.tile([P, PACK, P - VF, 4], F32)
-        quarter_sum = keep.tile([P, PACK, P - VF, 2], F32)
         f_codes = keep.tile([P, 256], U32, align_bytes=64)
         f_scales = keep.tile([P, 256], U8, align_bytes=64)
         o_codes = keep.tile([P, NCH * CH], U32, align_bytes=64)
@@ -84,16 +85,15 @@ def tile_correlationblock_t_kernel(tc, ok, fk, out_0, out_1):
                     out=fgrp[:, mt * P:mt * P + ng, j0:j0 + nj].rearrange("p g j -> p j g"),
                     in_=fk_at[q][:, :, 0:ng * 8].rearrange("p j (g d) -> p j g d", d=8), axis=AX.X, op=ALU.add)
 
-        def fsum_gpsimd_first(q):
+        def fsum_tensor(q):
             mt, j0, nj = FK_PIECES[q]
             src = fk_at[q][:, :, VF * 8:1024].rearrange("p j (g d) -> p j g d", d=8)
-            nc.gpsimd.tensor_tensor(out=half_sum[:, j0:j0 + nj], in0=src[:, :, :, 0:4], in1=src[:, :, :, 4:8], op=ALU.add)
+            for e in range(8):
+                nc.tensor.matmul(out=fs_ps[:, 0:4 * (P - VF)].rearrange("p (j g) -> p j g", j=4)[:, j0:j0 + nj], lhsT=ident[:],
+                                 rhs=src[:, :, :, e], start=e == 0, stop=e == 7)
 
-        def fsum_gpsimd_rest():
-            nc.gpsimd.tensor_tensor(out=quarter_sum[:], in0=half_sum[:, :, :, 0:2], in1=half_sum[:, :, :, 2:4], op=ALU.add)
-            with nc.allow_low_precision(reason="float32 sum, rounded once to bfloat16 as the task says"):
-                nc.gpsimd.tensor_tensor(out=fgrp[:, VF:P, :].rearrange("p g j -> p j g"),
-                                        in0=quarter_sum[:, :, :, 0], in1=quarter_sum[:, :, :, 1], op=ALU.add)
+        def fsum_tensor_out():
+            nc.scalar.copy(out=fgrp[:, VF:P, :], in_=fs_ps[:, 0:4 * (P - VF)].rearrange("p (j g) -> p g j", j=4))
 
         def quant_f():
             nc.vector.quantize_mx(out=f_codes[:].bitcast(FP8X4), scales=f_scales[:], in_=fgrp[:].rearrange("p g j -> p (g j)"))
@@ -151,14 +151,15 @@ def tile_correlationblock_t_kernel(tc, ok, fk, out_0, out_1):
 
         jobs = [(c, mt) for cp in range(NCH // 2) for mt in range(2) for c in (2 * cp, 2 * cp + 1)]
 
+        fs_ps = ps_c.tile([P, CH], F32, name="acc")
         for q in range(3):
-            fsum_gpsimd_first(q)
-        fsum_gpsimd_rest()
+            fsum_tensor(q)
+        fsum_tensor_out()
         for q in range(5):
             fsum(q)
         regroup(0, "s")
-        quant_f()
         quant(0)
+        quant_f()
         ak_passes(0)
         regroup(1, "s")
         regroup(2, "v")

@@ -20,7 +20,7 @@ CH = 512
 NCH = 8
 
 OK_UNITS = (512, 1024, 1024, 1024, 512)
-VF = 64
+VF = (64, 96)
 FK_PIECES = ((0, 0, 1), (0, 1, 1), (0, 2, 2), (1, 0, 2), (1, 2, 2))
 
 
@@ -79,7 +79,7 @@ def tile_correlationblock_t_kernel(tc, ok, fk, out_0, out_1):
 
         def fsum(q):
             mt, j0, nj = FK_PIECES[q]
-            ng = VF if mt == 0 else P
+            ng = VF[mt]
             with nc.allow_low_precision(reason="float32 sum, rounded once to bfloat16 as the task says"):
                 nc.vector.tensor_reduce(
                     out=fgrp[:, mt * P:mt * P + ng, j0:j0 + nj].rearrange("p g j -> p j g"),
@@ -87,13 +87,15 @@ def tile_correlationblock_t_kernel(tc, ok, fk, out_0, out_1):
 
         def fsum_tensor(q):
             mt, j0, nj = FK_PIECES[q]
-            src = fk_at[q][:, :, VF * 8:1024].rearrange("p j (g d) -> p j g d", d=8)
+            ng = P - VF[mt]
+            src = fk_at[q][:, :, VF[mt] * 8:1024].rearrange("p j (g d) -> p j g d", d=8)
             for e in range(8):
-                nc.tensor.matmul(out=fs_ps[:, 0:4 * (P - VF)].rearrange("p (j g) -> p j g", j=4)[:, j0:j0 + nj], lhsT=ident[:],
+                nc.tensor.matmul(out=fs_ps[mt][:, 0:4 * ng].rearrange("p (j g) -> p j g", j=4)[:, j0:j0 + nj], lhsT=ident[:],
                                  rhs=src[:, :, :, e], start=e == 0, stop=e == 7)
 
-        def fsum_tensor_out():
-            nc.scalar.copy(out=fgrp[:, VF:P, :], in_=fs_ps[:, 0:4 * (P - VF)].rearrange("p (j g) -> p g j", j=4))
+        def fsum_tensor_out(mt):
+            nc.scalar.copy(out=fgrp[:, mt * P + VF[mt]:(mt + 1) * P, :],
+                           in_=fs_ps[mt][:, 0:4 * (P - VF[mt])].rearrange("p (j g) -> p g j", j=4))
 
         def quant_f():
             nc.vector.quantize_mx(out=f_codes[:].bitcast(FP8X4), scales=f_scales[:], in_=fgrp[:].rearrange("p g j -> p (g j)"))
@@ -149,38 +151,46 @@ def tile_correlationblock_t_kernel(tc, ok, fk, out_0, out_1):
                 nc.sync.dma_start(out=corr_v[mt * P:(mt + 1) * P, (c - 1) * CH:(c + 1) * CH],
                                   in_=corr_sb[mt][:, (c - 1) * CH:(c + 1) * CH])
 
-        jobs = [(c, mt) for cp in range(NCH // 2) for mt in range(2) for c in (2 * cp, 2 * cp + 1)]
+        jobs = [(0, 0), (0, 1), (1, 0), (1, 1)]
+        jobs += [(c, mt) for cp in range(1, NCH // 2) for mt in range(2) for c in (2 * cp, 2 * cp + 1)]
 
-        fs_ps = ps_c.tile([P, CH], F32, name="acc")
-        for q in range(3):
-            fsum_tensor(q)
-        fsum_tensor_out()
+        fs_ps = {}
+        for mt in range(2):
+            acc = ps_c.tile([P, CH], F32, name="acc")
+            fs_ps[mt] = acc
         for q in range(5):
+            fsum_tensor(q)
             fsum(q)
+        fsum_tensor_out(0)
         regroup(0, "s")
+        fsum_tensor_out(1)
         quant(0)
         quant_f()
+        for i in range(2):
+            corr_pass(*jobs[i])
         ak_passes(0)
-        regroup(1, "s")
+        regroup(1, "s", 0, 2)
+        for i in range(2):
+            corr_out(*jobs[i])
         regroup(2, "v")
-        quant(1)
-        ak_passes(1)
+        regroup(1, "v", 2, 4)
         quant(2)
         ak_passes(2)
+        quant(1)
+        ak_passes(1)
         regroup(4, "s")
         regroup(3, "v")
-        quant(4)
-        ak_passes(4)
         quant(3)
         ak_passes(3)
-        for i in range(4):
+        quant(4)
+        ak_passes(4)
+        for i in range(2, 6):
             corr_pass(*jobs[i])
         regroup(6, "s")
         regroup(7, "s", 0, 2)
-        corr_out(*jobs[0])
-        corr_out(*jobs[1])
+        corr_out(*jobs[2])
         ak_out(0, 0, 0)
-        ak_out(1, 0, 1)
+        corr_out(*jobs[3])
         regroup(5, "v")
         regroup(7, "v", 2, 4)
         quant(5)
@@ -189,19 +199,18 @@ def tile_correlationblock_t_kernel(tc, ok, fk, out_0, out_1):
         ak_passes(6)
         quant(7)
         ak_passes(7)
-        corr_pass(*jobs[4])
-        corr_pass(*jobs[5])
-        corr_out(*jobs[2], eng=nc.vector.tensor_copy)
+        corr_pass(*jobs[6])
+        ak_out_vector(1, 0, 1)
         ak_out(0, 1, 2)
         ak_out_vector(1, 1, 3)
-        corr_out(*jobs[3], eng=nc.vector.tensor_copy)
+        corr_out(*jobs[4], eng=nc.vector.tensor_copy)
 
         mean_ps = ps_c.tile([P, CH], F32, name="acc")
         nc.tensor.matmul(out=mean_ps[:, 0:4], lhsT=ones[:], rhs=rowsum[:], start=True, stop=True)
         nc.vector.tensor_reduce(out=avg[:], in_=mean_ps[:, 0:4], axis=AX.X, op=ALU.add)
 
-        corr_pass(*jobs[6])
-        for i in range(4, 16):
+        corr_pass(*jobs[7])
+        for i in range(5, 16):
             corr_out(*jobs[i])
             if i + 3 < 16:
                 corr_pass(*jobs[i + 3])
@@ -212,6 +221,7 @@ def tile_correlationblock_t_kernel(tc, ok, fk, out_0, out_1):
         mn = keep.tile([P, 32], F32)
         mxm = keep.tile([P, 32], F32)
         inv = keep.tile([P, 32], F32)
+        off = keep.tile([P, 32], F32)
         mask = keep.tile([P, 512], F32)
 
         def select(i):
@@ -232,17 +242,27 @@ def tile_correlationblock_t_kernel(tc, ok, fk, out_0, out_1):
             nc.vector.tensor_reduce(out=out[:, i0 * 8:i1 * 8], in_=m[:, i0 * 512:i1 * 512].rearrange("p (k h) -> p k h", h=64),
                                     axis=AX.X, op=op)
 
-        def spread(g):
-            nc.vector.tensor_tensor(out=inv[:, g * 16:(g + 1) * 16], in0=mxm[:, g * 16:(g + 1) * 16],
-                                    in1=mn[:, g * 16:(g + 1) * 16], op=ALU.subtract)
+        def spread(i0, i1):
+            cols = slice(i0 * 8, i1 * 8)
+            nc.vector.tensor_tensor(out=inv[:, cols], in0=mxm[:, cols], in1=mn[:, cols], op=ALU.subtract)
 
-        def recip(g):
-            nc.vector.reciprocal(out=inv[:, g * 16:(g + 1) * 16], in_=inv[:, g * 16:(g + 1) * 16])
+        def recip(i0, i1):
+            cols = slice(i0 * 8, i1 * 8)
+            nc.vector.reciprocal(out=inv[:, cols], in_=inv[:, cols])
+
+        def offset(i0, i1):
+            cols = slice(i0 * 8, i1 * 8)
+            nc.vector.scalar_tensor_tensor(out=off[:, cols], in0=mn[:, cols], scalar=-1.0, in1=inv[:, cols], op0=ALU.mult, op1=ALU.mult)
 
         def normalise(i):
             for c in range(i * 8, (i + 1) * 8):
                 run = m[:, c * 64:(c + 1) * 64]
                 nc.vector.tensor_scalar(out=run, in0=run, scalar1=mn[:, c:c + 1], scalar2=inv[:, c:c + 1], op0=ALU.subtract, op1=ALU.mult)
+
+        def normalise_scalar(i):
+            for c in range(i * 8, (i + 1) * 8):
+                run = m[:, c * 64:(c + 1) * 64]
+                nc.scalar.activation(out=run, in_=run, func=ACT.Identity, scale=inv[:, c:c + 1], bias=off[:, c:c + 1])
 
         def reorder(i, copy):
             copy(out=hat[i][:].rearrange("p (b i k) -> p b k i", i=4, k=8),
@@ -255,26 +275,29 @@ def tile_correlationblock_t_kernel(tc, ok, fk, out_0, out_1):
         select(0)
         select_gpsimd(3)
         select(1)
-        select(2)
         extreme(mn, ALU.min, 0, 1)
+        extreme(mxm, ALU.max, 0, 1)
+        select(2)
         extreme(mn, ALU.min, 1, 2)
-        extreme(mxm, ALU.max, 0, 2)
+        extreme(mxm, ALU.max, 1, 2)
         extreme(mn, ALU.min, 2, 3)
-        spread(0)
+        spread(0, 2)
         extreme(mxm, ALU.max, 2, 3)
-        recip(0)
+        recip(0, 2)
         extreme(mn, ALU.min, 3, 4)
+        offset(1, 2)
         normalise(0)
+        spread(2, 3)
+        reorder(0, nc.vector.tensor_copy)
+        recip(2, 3)
         extreme(mxm, ALU.max, 3, 4)
-        normalise(1)
-        spread(1)
-        for i in range(2):
-            reorder(i, nc.scalar.copy)
-            store(i)
-        recip(1)
-        normalise(2)
-        reorder(2, nc.scalar.copy)
-        store(2)
+        offset(2, 3)
+        spread(3, 4)
+        recip(3, 4)
         normalise(3)
         reorder(3, nc.vector.tensor_copy)
-        store(3)
+        for i in range(1, 3):
+            normalise_scalar(i)
+            reorder(i, nc.scalar.copy)
+        for i in (0, 1, 3, 2):
+            store(i)

from contextlib import ExitStack

import concourse.mybir as mybir
from concourse.masks import make_identity

FLOPS = 2 * 512 * 256 * 4096

F32 = mybir.dt.float32
BF16 = mybir.dt.bfloat16
U32 = mybir.dt.uint32
U8 = mybir.dt.uint8
FP8X4 = mybir.dt.float8_e4m3fn_x4
ALU = mybir.AluOpType
ACT = mybir.ActivationFunctionType
AX = mybir.AxisListType

P = 128
PACK = 4
CH = 512
NCH = 8

OK_UNITS = (512, 1024, 1024, 1024, 512)
VF = (64, 96)
FK_PIECES = ((0, 0, 1), (0, 1, 1), (0, 2, 2), (1, 0, 2), (1, 2, 2))


def tile_correlationblock_t_kernel(tc, ok, fk, out_0, out_1):
    nc = tc.nc
    ok_v = ok.rearrange("(p j) x y z -> p j (x y z)", j=PACK)
    fk_v = fk.rearrange("(p j) h w d -> p j (h w d)", j=PACK)
    corr_v = out_0.rearrange("(r s) h w k -> r (s h w k)", s=2)
    hat_v = out_1.rearrange("(r s) h k -> r (s h k)", s=2)

    with ExitStack() as ctx:
        keep = ctx.enter_context(tc.tile_pool(name="keep", bufs=1))
        ps_ak = ctx.enter_context(tc.psum_pool(name="ps_ak", bufs=1))
        ps_c = ctx.enter_context(tc.psum_pool(name="ps_c", bufs=4))
        ctx.enter_context(tc.manual_schedule())

        ones = keep.tile([P, P], F32)
        nc.vector.memset(ones[:], 1.0 / 262144.0)
        ident = keep.tile([P, P], BF16)
        make_identity(nc, ident[:])

        fk_at = {}
        ok_at = {}

        def load(view, units, u, table, step, nm):
            lo = sum(units[:u])
            t = keep.tile([P, PACK, units[u]], BF16, name="%s%d" % (nm, u))
            nc.sync.dma_start(out=t[:], in_=view[:, :, lo:lo + units[u]])
            for i in range(units[u] // step):
                table[lo // step + i] = t[:, :, i * step:(i + 1) * step]

        def load_fk(q):
            mt, j0, nj = FK_PIECES[q]
            t = keep.tile([P, nj, 1024], BF16, name="fk_raw%d" % q)
            nc.sync.dma_start(out=t[:], in_=fk_v[:, j0:j0 + nj, mt * 1024:(mt + 1) * 1024])
            fk_at[q] = t

        for q in range(4):
            load_fk(q)
        load(ok_v, OK_UNITS, 0, ok_at, CH, "ok_raw")
        load_fk(4)
        for u in range(1, len(OK_UNITS)):
            load(ok_v, OK_UNITS, u, ok_at, CH, "ok_raw")

        fgrp = keep.tile([P, 256, PACK], BF16, align_bytes=64)
        f_codes = keep.tile([P, 256], U32, align_bytes=64)
        f_scales = keep.tile([P, 256], U8, align_bytes=64)
        o_codes = keep.tile([P, NCH * CH], U32, align_bytes=64)
        o_scales = keep.tile([P, NCH * CH], U8, align_bytes=64)
        grp = [keep.tile([P, CH, PACK], BF16, name="grp%d" % c, align_bytes=64) for c in range(NCH)]
        corr_sb = [keep.tile([P, NCH * CH], F32, name="corr_sb%d" % mt) for mt in range(2)]
        ak_sb = [keep.tile([P, 1024], F32, name="ak_sb%d" % mt) for mt in range(2)]
        ak_ps = [[ps_ak.tile([P, 512], F32, name="ak_ps%d%d" % (mt, s)) for s in range(2)] for mt in range(2)]
        rowsum = keep.tile([P, 4], F32)
        avg = keep.tile([P, 1], F32)

        def fsum(q):
            mt, j0, nj = FK_PIECES[q]
            ng = VF[mt]
            with nc.allow_low_precision(reason="float32 sum, rounded once to bfloat16 as the task says"):
                nc.vector.tensor_reduce(
                    out=fgrp[:, mt * P:mt * P + ng, j0:j0 + nj].rearrange("p g j -> p j g"),
                    in_=fk_at[q][:, :, 0:ng * 8].rearrange("p j (g d) -> p j g d", d=8), axis=AX.X, op=ALU.add)

        def fsum_tensor(q):
            mt, j0, nj = FK_PIECES[q]
            ng = P - VF[mt]
            src = fk_at[q][:, :, VF[mt] * 8:1024].rearrange("p j (g d) -> p j g d", d=8)
            for e in range(8):
                nc.tensor.matmul(out=fs_ps[mt][:, 0:4 * ng].rearrange("p (j g) -> p j g", j=4)[:, j0:j0 + nj], lhsT=ident[:],
                                 rhs=src[:, :, :, e], start=e == 0, stop=e == 7)

        def fsum_tensor_out(mt):
            nc.scalar.copy(out=fgrp[:, mt * P + VF[mt]:(mt + 1) * P, :],
                           in_=fs_ps[mt][:, 0:4 * (P - VF[mt])].rearrange("p (j g) -> p g j", j=4))

        def quant_f():
            nc.vector.quantize_mx(out=f_codes[:].bitcast(FP8X4), scales=f_scales[:], in_=fgrp[:].rearrange("p g j -> p (g j)"))

        def regroup(c, eng, w0=0, w1=4):
            src = ok_at[c].rearrange("p j (h w k) -> p w h j k", w=4, k=8)[:, w0:w1]
            dst = grp[c][:].rearrange("p (w h k) j -> p w h j k", w=4, k=8)[:, w0:w1]
            if eng == "v":
                nc.vector.tensor_copy(out=dst, in_=src)
            else:
                for w in range(w1 - w0):
                    nc.scalar.copy(out=dst[:, w], in_=src[:, w])

        def quant(c):
            nc.vector.quantize_mx(
                out=o_codes[:, c * CH:(c + 1) * CH].bitcast(FP8X4), scales=o_scales[:, c * CH:(c + 1) * CH],
                in_=grp[c][:].rearrange("p c j -> p (c j)"))

        def mx(out, mt, lo, n, start, stop):
            nc.tensor.matmul_mx(
                out=out, lhsT=f_codes[:, mt * P:(mt + 1) * P].bitcast(FP8X4), lhsT_scale=f_scales[:, mt * P:(mt + 1) * P],
                rhs=o_codes[:, lo:lo + n].bitcast(FP8X4), rhs_scale=o_scales[:, lo:lo + n], start=start, stop=stop)

        def ak_passes(c):
            for mt in range(2):
                for w in range(4):
                    mx(ak_ps[mt][c // 4][:, (c % 4) * P:(c % 4 + 1) * P], mt, c * CH + w * P, P, w == 0, w == 3)

        def ak_out(mt, s, col):
            nc.scalar.activation(
                out=ak_sb[mt][:, s * 512:(s + 1) * 512].rearrange("p (k h) -> p k h", k=8),
                in_=ak_ps[mt][s][:].rearrange("p (h k) -> p k h", k=8), func=ACT.Copy,
                accum_out=rowsum[:, col:col + 1])

        def ak_out_vector(mt, s, col):
            nc.vector.tensor_scalar(
                out=ak_sb[mt][:, s * 512:(s + 1) * 512].rearrange("p (k h) -> p k h", k=8),
                in0=ak_ps[mt][s][:].rearrange("p (h k) -> p k h", k=8), scalar1=1.0, scalar2=0.0, op0=ALU.mult, op1=ALU.add,
                accum_out=rowsum[:, col:col + 1])

        banks = {}

        def corr_pass(c, mt):
            acc = ps_c.tile([P, CH], F32, name="acc")
            banks[(c, mt)] = acc
            mx(acc[:], mt, c * CH, CH, True, True)

        def corr_out(c, mt, eng=None):
            (eng or nc.scalar.copy)(
                out=corr_sb[mt][:, c * CH:(c + 1) * CH].rearrange("p (h w k) -> p h w k", w=4, k=8),
                in_=banks[(c, mt)][:].rearrange("p (w h k) -> p h w k", w=4, k=8))
            if c % 2 == 1:
                nc.sync.dma_start(out=corr_v[mt * P:(mt + 1) * P, (c - 1) * CH:(c + 1) * CH],
                                  in_=corr_sb[mt][:, (c - 1) * CH:(c + 1) * CH])

        jobs = [(0, 0), (0, 1), (1, 0), (1, 1)]
        jobs += [(c, mt) for cp in range(1, NCH // 2) for mt in range(2) for c in (2 * cp, 2 * cp + 1)]

        fs_ps = {}
        for mt in range(2):
            acc = ps_c.tile([P, CH], F32, name="acc")
            fs_ps[mt] = acc
        for q in range(5):
            fsum_tensor(q)
            fsum(q)
        fsum_tensor_out(0)
        regroup(0, "s")
        fsum_tensor_out(1)
        quant(0)
        quant_f()
        for i in range(2):
            corr_pass(*jobs[i])
        ak_passes(0)
        regroup(1, "s", 0, 2)
        for i in range(2):
            corr_out(*jobs[i])
        regroup(2, "v")
        regroup(1, "v", 2, 4)
        quant(2)
        ak_passes(2)
        quant(1)
        ak_passes(1)
        regroup(4, "s")
        regroup(3, "v")
        quant(3)
        ak_passes(3)
        quant(4)
        ak_passes(4)
        for i in range(2, 6):
            corr_pass(*jobs[i])
        regroup(6, "s")
        regroup(7, "s", 0, 2)
        corr_out(*jobs[2])
        ak_out(0, 0, 0)
        corr_out(*jobs[3])
        regroup(5, "v")
        regroup(7, "v", 2, 4)
        quant(5)
        ak_passes(5)
        quant(6)
        ak_passes(6)
        quant(7)
        ak_passes(7)
        corr_pass(*jobs[6])
        ak_out_vector(1, 0, 1)
        ak_out(0, 1, 2)
        ak_out_vector(1, 1, 3)
        corr_out(*jobs[4], eng=nc.vector.tensor_copy)

        mean_ps = ps_c.tile([P, CH], F32, name="acc")
        nc.tensor.matmul(out=mean_ps[:, 0:4], lhsT=ones[:], rhs=rowsum[:], start=True, stop=True)
        nc.vector.tensor_reduce(out=avg[:], in_=mean_ps[:, 0:4], axis=AX.X, op=ALU.add)

        corr_pass(*jobs[7])
        for i in range(5, 16):
            corr_out(*jobs[i])
            if i + 3 < 16:
                corr_pass(*jobs[i + 3])

        pieces = [(0, 0), (1, 0), (0, 1), (1, 1)]
        m = keep.tile([P, 2048], F32)
        hat = [keep.tile([P, 512], F32, name="hat%d" % i) for i in range(4)]
        mn = keep.tile([P, 32], F32)
        mxm = keep.tile([P, 32], F32)
        inv = keep.tile([P, 32], F32)
        off = keep.tile([P, 32], F32)
        mask = keep.tile([P, 512], F32)

        def select(i):
            mt, s = pieces[i]
            nc.vector.scalar_tensor_tensor(
                out=m[:, i * 512:(i + 1) * 512].rearrange("p (k h) -> p k h", k=8),
                in0=ak_ps[mt][s][:].rearrange("p (h k) -> p k h", k=8),
                scalar=avg[:, 0:1], in1=ak_sb[mt][:, s * 512:(s + 1) * 512].rearrange("p (k h) -> p k h", k=8),
                op0=ALU.is_gt, op1=ALU.mult)

        def select_gpsimd(i):
            mt, s = pieces[i]
            ak = ak_sb[mt][:, s * 512:(s + 1) * 512]
            nc.gpsimd.tensor_scalar(out=mask[:], in0=ak, scalar1=avg[:, 0:1], scalar2=1.0, op0=ALU.is_gt, op1=ALU.mult)
            nc.gpsimd.tensor_tensor(out=m[:, i * 512:(i + 1) * 512], in0=mask[:], in1=ak, op=ALU.mult)

        def extreme(out, op, i0, i1):
            nc.vector.tensor_reduce(out=out[:, i0 * 8:i1 * 8], in_=m[:, i0 * 512:i1 * 512].rearrange("p (k h) -> p k h", h=64),
                                    axis=AX.X, op=op)

        def spread(i0, i1):
            cols = slice(i0 * 8, i1 * 8)
            nc.vector.tensor_tensor(out=inv[:, cols], in0=mxm[:, cols], in1=mn[:, cols], op=ALU.subtract)

        def recip(i0, i1):
            cols = slice(i0 * 8, i1 * 8)
            nc.vector.reciprocal(out=inv[:, cols], in_=inv[:, cols])

        def offset(i0, i1):
            cols = slice(i0 * 8, i1 * 8)
            nc.vector.scalar_tensor_tensor(out=off[:, cols], in0=mn[:, cols], scalar=-1.0, in1=inv[:, cols], op0=ALU.mult, op1=ALU.mult)

        def normalise(i):
            for c in range(i * 8, (i + 1) * 8):
                run = m[:, c * 64:(c + 1) * 64]
                nc.vector.tensor_scalar(out=run, in0=run, scalar1=mn[:, c:c + 1], scalar2=inv[:, c:c + 1], op0=ALU.subtract, op1=ALU.mult)

        def normalise_scalar(i):
            for c in range(i * 8, (i + 1) * 8):
                run = m[:, c * 64:(c + 1) * 64]
                nc.scalar.activation(out=run, in_=run, func=ACT.Identity, scale=inv[:, c:c + 1], bias=off[:, c:c + 1])

        def reorder(i, copy):
            copy(out=hat[i][:].rearrange("p (b i k) -> p b k i", i=4, k=8),
                 in_=m[:, i * 512:(i + 1) * 512].rearrange("p (k b i) -> p b k i", k=8, i=4))

        def store(i):
            mt, s = pieces[i]
            nc.sync.dma_start(out=hat_v[mt * P:(mt + 1) * P, s * 512:(s + 1) * 512], in_=hat[i][:])

        select(0)
        select_gpsimd(3)
        select(1)
        extreme(mn, ALU.min, 0, 1)
        extreme(mxm, ALU.max, 0, 1)
        select(2)
        extreme(mn, ALU.min, 1, 2)
        extreme(mxm, ALU.max, 1, 2)
        extreme(mn, ALU.min, 2, 3)
        spread(0, 2)
        extreme(mxm, ALU.max, 2, 3)
        recip(0, 2)
        extreme(mn, ALU.min, 3, 4)
        offset(1, 2)
        normalise(0)
        spread(2, 3)
        reorder(0, nc.vector.tensor_copy)
        recip(2, 3)
        extreme(mxm, ALU.max, 3, 4)
        offset(2, 3)
        spread(3, 4)
        recip(3, 4)
        normalise(3)
        reorder(3, nc.vector.tensor_copy)
        for i in range(1, 3):
            normalise_scalar(i)
            reorder(i, nc.scalar.copy)
        for i in (0, 1, 3, 2):
            store(i)
